import numpy as np
import ml_dtypes


def mxq(x, axis, fmt="e4m3"):
    dtype, down = {"e4m3": (ml_dtypes.float8_e4m3fn, 7), "e5m2": (ml_dtypes.float8_e5m2, 14)}[fmt]
    v = np.moveaxis(np.asarray(x, np.float32).astype(ml_dtypes.bfloat16).astype(np.float64), axis, -1)
    blocks = v.reshape(v.shape[:-1] + (-1, 32))
    amax = np.abs(blocks).max(-1, keepdims=True)
    byte = np.maximum(np.where(amax > 0, np.frexp(amax)[1] - 1 + 127, 0) - down, 1)
    scale = np.exp2(byte - 127.0)
    codes = (blocks / scale).astype(np.float32).astype(dtype).astype(np.float64)
    return np.moveaxis((codes * scale).reshape(v.shape), -1, axis)


WIDE = False


def mx_kscale(k):
    if not WIDE:
        return np.ones(k)
    levels = np.array([20, -20, 10, -10, 0])
    a = np.random.permutation(np.resize(levels, k // 512 * 4)).reshape(k // 512, 4)
    idx = np.arange(k)
    return np.exp2(a[idx // 512, idx % 128 // 32])


BF16 = ml_dtypes.bfloat16


def bf(x):
    return np.asarray(x, np.float32).astype(BF16)


def f64(x):
    return np.asarray(x).astype(np.float64)


B, H, W, CIN, COUT = 512, 2, 2, 1024, 512
P = H * W


def _diag_blocks(kernel):
    k4 = f64(kernel).reshape(P, CIN, P, COUT)
    idx = np.arange(P)
    return k4[idx, :, idx, :]


def setup_inputs():
    u = mx_kscale(COUT)
    inputs = np.random.standard_normal((B, H, W, CIN))
    kernel = np.random.standard_normal((H, W, CIN, H, W, COUT)) / np.sqrt(CIN) / u
    bias = np.random.standard_normal((H, W, COUT)) * 0.5
    g = np.random.standard_normal((B, H, W, COUT)) * np.exp2(np.random.randint(-12, 1, (B, H, W, 1))) * 32.0 * u
    return {"inputs": bf(inputs), "kernel": bf(kernel), "bias": bf(bias), "grad_out": bf(g)}


def reference(inputs, kernel, bias, grad_out):
    g = f64(grad_out).reshape(B, P, COUT).transpose(1, 0, 2)
    kd = _diag_blocks(kernel)
    gx = mxq(g, 2, "e5m2") @ mxq(kd, 2, "e4m3").transpose(0, 2, 1)
    return gx.transpose(1, 0, 2).reshape(B, H, W, CIN)

@@ -1,0 +1,154 @@
+from contextlib import ExitStack
+
+import concourse.mybir as mybir
+from concourse.masks import make_identity
+
+F32 = mybir.dt.float32
+BF16 = mybir.dt.bfloat16
+U32 = mybir.dt.uint32
+U8 = mybir.dt.uint8
+E4M3X4 = mybir.dt.float8_e4m3fn_x4
+E5M2X4 = mybir.dt.float8_e5m2_x4
+
+P = 128
+B, PLACES, CIN, COUT = 512, 4, 1024, 512
+FLOPS = 2 * PLACES * B * CIN * COUT
+BYTES = 2 * B * PLACES * COUT + 2 * PLACES * CIN * COUT + 4 * B * PLACES * CIN
+
+PIN = True
+UNIT_ROWS = 512
+
+
+def tile_locallyconnected2d_t_kernel(tc, inputs, kernel, bias, grad_out, out):
+    nc = tc.nc
+    g_rows = grad_out.rearrange("b i j o -> b (i j o)")
+    k_blocks = kernel.rearrange("i j c k l o -> (i j) c (k l) o")
+    out_rows = out.rearrange("b i j c -> b (i j c)")
+
+    units = [("g", 0), ("g", 1)] + [("k", h) for h in range(8)] + [("g", 2), ("g", 3)]
+    n = len(units)
+    unit_of = {}
+    for i, u in enumerate(units):
+        unit_of[u] = i
+
+    with ExitStack() as ctx:
+        if PIN:
+            ctx.enter_context(tc.manual_schedule())
+        const = ctx.enter_context(tc.tile_pool(name="const", bufs=1))
+        rawp = ctx.enter_context(tc.tile_pool(name="rawp", bufs=1))
+        keep = ctx.enter_context(tc.tile_pool(name="keep", bufs=1))
+        stage = ctx.enter_context(tc.tile_pool(name="stage", bufs=4))
+        outp = ctx.enter_context(tc.tile_pool(name="outp", bufs=1))
+        tpsum = ctx.enter_context(tc.psum_pool(name="tpsum", bufs=4))
+        mpsum = ctx.enter_context(tc.psum_pool(name="mpsum", bufs=4))
+
+        raw, codes, scales = [], [], []
+        for i, (kind, idx) in enumerate(units):
+            raw_i = rawp.tile([P, 4 * UNIT_ROWS], BF16, name="raw%d" % i)
+            raw.append(raw_i)
+            if kind == "g":
+                nc.sync.dma_start(out=raw_i[:], in_=g_rows[P * idx : P * (idx + 1), :])
+            else:
+                place, half = divmod(idx, 2)
+                rows = k_blocks[place, UNIT_ROWS * half : UNIT_ROWS * (half + 1), place, :]
+                nc.sync.dma_start(
+                    out=raw_i[:].rearrange("q (t o) -> q t o", t=4),
+                    in_=rows.rearrange("(t q) o -> q t o", q=P),
+                )
+            codes_i = keep.tile([P, UNIT_ROWS], U32, name="codes%d" % i, align_bytes=64)
+            scales_i = keep.tile([P, UNIT_ROWS], U8, name="scales%d" % i, align_bytes=64)
+            codes.append(codes_i)
+            scales.append(scales_i)
+
+        ident = const.tile([P, P], F32, name="ident")
+        make_identity(nc, ident[:])
+
+        dest = {}
+        out_tiles = {}
+        for t in range(4):
+            if t < 2:
+                for pair in range(2):
+                    o = outp.tile([P, 2 * CIN], F32, name="out%d_%d" % (t, pair))
+                    out_tiles[(t, pair)] = o
+                    for s in range(2):
+                        dest[(t, 2 * pair + s)] = (o, s * CIN)
+            else:
+                o = outp.tile([P, PLACES * CIN], F32, name="out%d" % t)
+                out_tiles[(t, 0)] = o
+                for place in range(PLACES):
+                    dest[(t, place)] = (o, place * CIN)
+
+        booked = {"v": 0, "s": 0}
+
+        def copy_out(dst, src, engine=None):
+            if engine is None:
+                engine = "s" if booked["s"] <= booked["v"] else "v"
+            booked[engine] = booked[engine] + 1
+            if engine == "v":
+                nc.vector.tensor_copy(out=dst, in_=src)
+            else:
+                nc.scalar.copy(out=dst, in_=src)
+
+        grouped_of = {}
+
+        def prep(i):
+            words = raw[i][:].bitcast(F32)
+            grouped = stage.tile([P, 4 * UNIT_ROWS], BF16, name="grouped", tag="grouped", align_bytes=64)
+            grouped_of[i] = grouped
+            gw = grouped[:].bitcast(F32).rearrange("p (r u) -> p r u", u=2)
+            for j in range(2):
+                xt = tpsum.tile([P, 2, 2 * P], F32, name="xt", tag="xt")
+                for s in range(2):
+                    for u in range(2):
+                        first = 256 * (2 * j + s) + P * u
+                        nc.tensor.transpose(xt[:, u, P * s : P * (s + 1)], words[:, first : first + P], ident[:])
+                copy_out(gw[:, 256 * j : 256 * (j + 1), :], xt[:].rearrange("p u r -> p r u"), "v" if j == 0 else "s")
+
+        def quantise(i):
+            fmt = E5M2X4 if units[i][0] == "g" else E4M3X4
+            booked["v"] = booked["v"] + 1
+            nc.vector.quantize_mx(out=codes[i][:].bitcast(fmt), scales=scales[i][:], in_=grouped_of[i][:])
+
+        def product(t, h):
+            gi, ki = unit_of[("g", t)], unit_of[("k", h)]
+            place, half = divmod(h, 2)
+            cols = slice(P * place, P * (place + 1))
+            acc = mpsum.tile([P, UNIT_ROWS], F32, name="acc", tag="acc")
+            nc.tensor.matmul_mx(
+                out=acc[:],
+                lhsT=codes[gi][:, cols].bitcast(E5M2X4),
+                lhsT_scale=scales[gi][:, cols],
+                rhs=codes[ki][:].bitcast(E4M3X4),
+                rhs_scale=scales[ki][:],
+                start=True,
+                stop=True,
+            )
+            o, first = dest[(t, place)]
+            first = first + UNIT_ROWS * half
+            copy_out(o[:, first : first + UNIT_ROWS], acc[:])
+
+        def store(t, pair):
+            o = out_tiles[(t, pair)]
+            width = o.shape[1]
+            nc.sync.dma_start(out=out_rows[P * t : P * (t + 1), width * pair : width * (pair + 1)], in_=o[:])
+
+        def products_after(i):
+            kind, idx = units[i]
+            if kind == "k":
+                for t in range(2):
+                    product(t, idx)
+                if idx % 4 == 3:
+                    for t in range(2):
+                        store(t, idx // 4)
+            elif idx >= 2:
+                for h in range(8):
+                    product(idx, h)
+                store(idx, 0)
+
+        for i in range(n + 2):
+            if i < n:
+                prep(i)
+            if 1 <= i <= n:
+                quantise(i - 1)
+            if i >= 2:
+                products_after(i - 2)

@@ -66,17 +66,11 @@ def tile_locallyconnected2d_t_kernel(tc, inputs, kernel, bias, grad_out, out):
         dest = {}
         out_tiles = {}
         for t in range(4):
-            if t < 2:
-                for pair in range(2):
-                    o = outp.tile([P, 2 * CIN], F32, name="out%d_%d" % (t, pair))
-                    out_tiles[(t, pair)] = o
-                    for s in range(2):
-                        dest[(t, 2 * pair + s)] = (o, s * CIN)
-            else:
-                o = outp.tile([P, PLACES * CIN], F32, name="out%d" % t)
-                out_tiles[(t, 0)] = o
-                for place in range(PLACES):
-                    dest[(t, place)] = (o, place * CIN)
+            for pair in range(2):
+                o = outp.tile([P, 2 * CIN], F32, name="out%d_%d" % (t, pair))
+                out_tiles[(t, pair)] = o
+                for s in range(2):
+                    dest[(t, 2 * pair + s)] = (o, s * CIN)
 
         booked = {"v": 0, "s": 0}
 
@@ -143,7 +137,8 @@ def tile_locallyconnected2d_t_kernel(tc, inputs, kernel, bias, grad_out, out):
             elif idx >= 2:
                 for h in range(8):
                     product(idx, h)
-                store(idx, 0)
+                    if h % 4 == 3:
+                        store(idx, h // 4)
 
         for i in range(n + 2):
             if i < n:

@@ -25,7 +25,8 @@ def tile_locallyconnected2d_t_kernel(tc, inputs, kernel, bias, grad_out, out):
     k_blocks = kernel.rearrange("i j c k l o -> (i j) c (k l) o")
     out_rows = out.rearrange("b i j c -> b (i j c)")
 
-    units = [("g", 0), ("g", 1)] + [("k", h) for h in range(8)] + [("g", 2), ("g", 3)]
+    units = [("g", 0), ("g", 1)] + [("k", h) for h in (0, 2, 1, 3, 4, 6, 5, 7)] + [("g", 2), ("g", 3)]
+    on_scalar_queue = (("g", 1), ("k", 2), ("k", 3), ("k", 6))
     n = len(units)
     unit_of = {}
     for i, u in enumerate(units):
@@ -46,12 +47,13 @@ def tile_locallyconnected2d_t_kernel(tc, inputs, kernel, bias, grad_out, out):
         for i, (kind, idx) in enumerate(units):
             raw_i = rawp.tile([P, 4 * UNIT_ROWS], BF16, name="raw%d" % i)
             raw.append(raw_i)
+            queue = nc.scalar if (kind, idx) in on_scalar_queue else nc.sync
             if kind == "g":
-                nc.sync.dma_start(out=raw_i[:], in_=g_rows[P * idx : P * (idx + 1), :])
+                queue.dma_start(out=raw_i[:], in_=g_rows[P * idx : P * (idx + 1), :])
             else:
                 place, half = divmod(idx, 2)
                 rows = k_blocks[place, UNIT_ROWS * half : UNIT_ROWS * (half + 1), place, :]
-                nc.sync.dma_start(
+                queue.dma_start(
                     out=raw_i[:].rearrange("q (t o) -> q t o", t=4),
                     in_=rows.rearrange("(t q) o -> q t o", q=P),
                 )
@@ -66,11 +68,17 @@ def tile_locallyconnected2d_t_kernel(tc, inputs, kernel, bias, grad_out, out):
         dest = {}
         out_tiles = {}
         for t in range(4):
-            for pair in range(2):
-                o = outp.tile([P, 2 * CIN], F32, name="out%d_%d" % (t, pair))
-                out_tiles[(t, pair)] = o
-                for s in range(2):
-                    dest[(t, 2 * pair + s)] = (o, s * CIN)
+            if t < 2:
+                for pair in range(2):
+                    o = outp.tile([P, 2 * CIN], F32, name="out%d_%d" % (t, pair))
+                    out_tiles[(t, pair)] = o
+                    for s in range(2):
+                        dest[(t, 2 * pair + s)] = (o, s * CIN)
+            else:
+                o = outp.tile([P, PLACES * CIN], F32, name="out%d" % t)
+                out_tiles[(t, 0)] = o
+                for place in range(PLACES):
+                    dest[(t, place)] = (o, place * CIN)
 
         booked = {"v": 0, "s": 0}
 
@@ -137,8 +145,7 @@ def tile_locallyconnected2d_t_kernel(tc, inputs, kernel, bias, grad_out, out):
             elif idx >= 2:
                 for h in range(8):
                     product(idx, h)
-                    if h % 4 == 3:
-                        store(idx, h // 4)
+                store(idx, 0)
 
         for i in range(n + 2):
             if i < n:

@@ -16,6 +16,7 @@ FLOPS = 2 * PLACES * B * CIN * COUT
 BYTES = 2 * B * PLACES * COUT + 2 * PLACES * CIN * COUT + 4 * B * PLACES * CIN
 
 PIN = True
+PLACES_PER_STORE = (1, 1, 2, 4)
 UNIT_ROWS = 512
 
 
@@ -25,8 +26,7 @@ def tile_locallyconnected2d_t_kernel(tc, inputs, kernel, bias, grad_out, out):
     k_blocks = kernel.rearrange("i j c k l o -> (i j) c (k l) o")
     out_rows = out.rearrange("b i j c -> b (i j c)")
 
-    units = [("g", 0), ("g", 1)] + [("k", h) for h in (0, 2, 1, 3, 4, 6, 5, 7)] + [("g", 2), ("g", 3)]
-    on_scalar_queue = (("g", 1), ("k", 2), ("k", 3), ("k", 6))
+    units = [("g", 0), ("g", 1)] + [("k", h) for h in range(8)] + [("g", 2), ("g", 3)]
     n = len(units)
     unit_of = {}
     for i, u in enumerate(units):
@@ -47,13 +47,12 @@ def tile_locallyconnected2d_t_kernel(tc, inputs, kernel, bias, grad_out, out):
         for i, (kind, idx) in enumerate(units):
             raw_i = rawp.tile([P, 4 * UNIT_ROWS], BF16, name="raw%d" % i)
             raw.append(raw_i)
-            queue = nc.scalar if (kind, idx) in on_scalar_queue else nc.sync
             if kind == "g":
-                queue.dma_start(out=raw_i[:], in_=g_rows[P * idx : P * (idx + 1), :])
+                nc.sync.dma_start(out=raw_i[:], in_=g_rows[P * idx : P * (idx + 1), :])
             else:
                 place, half = divmod(idx, 2)
                 rows = k_blocks[place, UNIT_ROWS * half : UNIT_ROWS * (half + 1), place, :]
-                queue.dma_start(
+                nc.sync.dma_start(
                     out=raw_i[:].rearrange("q (t o) -> q t o", t=4),
                     in_=rows.rearrange("(t q) o -> q t o", q=P),
                 )
@@ -66,19 +65,11 @@ def tile_locallyconnected2d_t_kernel(tc, inputs, kernel, bias, grad_out, out):
         make_identity(nc, ident[:])
 
         dest = {}
-        out_tiles = {}
         for t in range(4):
-            if t < 2:
-                for pair in range(2):
-                    o = outp.tile([P, 2 * CIN], F32, name="out%d_%d" % (t, pair))
-                    out_tiles[(t, pair)] = o
-                    for s in range(2):
-                        dest[(t, 2 * pair + s)] = (o, s * CIN)
-            else:
-                o = outp.tile([P, PLACES * CIN], F32, name="out%d" % t)
-                out_tiles[(t, 0)] = o
-                for place in range(PLACES):
-                    dest[(t, place)] = (o, place * CIN)
+            for first_place in range(0, PLACES, PLACES_PER_STORE[t]):
+                o = outp.tile([P, PLACES_PER_STORE[t] * CIN], F32, name="out%d_%d" % (t, first_place))
+                for s in range(PLACES_PER_STORE[t]):
+                    dest[(t, first_place + s)] = (o, s * CIN)
 
         booked = {"v": 0, "s": 0}
 
@@ -128,24 +119,18 @@ def tile_locallyconnected2d_t_kernel(tc, inputs, kernel, bias, grad_out, out):
             o, first = dest[(t, place)]
             first = first + UNIT_ROWS * half
             copy_out(o[:, first : first + UNIT_ROWS], acc[:])
-
-        def store(t, pair):
-            o = out_tiles[(t, pair)]
-            width = o.shape[1]
-            nc.sync.dma_start(out=out_rows[P * t : P * (t + 1), width * pair : width * (pair + 1)], in_=o[:])
+            if first + UNIT_ROWS == o.shape[1]:
+                last = (place + 1) * CIN
+                nc.sync.dma_start(out=out_rows[P * t : P * (t + 1), last - o.shape[1] : last], in_=o[:])
 
         def products_after(i):
             kind, idx = units[i]
             if kind == "k":
                 for t in range(2):
                     product(t, idx)
-                if idx % 4 == 3:
-                    for t in range(2):
-                        store(t, idx // 4)
             elif idx >= 2:
                 for h in range(8):
                     product(idx, h)
-                store(idx, 0)
 
         for i in range(n + 2):
             if i < n:

@@ -45,7 +45,7 @@ def tile_locallyconnected2d_t_kernel(tc, inputs, kernel, bias, grad_out, out):
 
         raw, codes, scales = [], [], []
         for i, (kind, idx) in enumerate(units):
-            raw_i = rawp.tile([P, 4 * UNIT_ROWS], BF16, name="raw%d" % i)
+            raw_i = rawp.tile([P, 4 * UNIT_ROWS], BF16, name="raw%d" % i, align_bytes=256)
             raw.append(raw_i)
             if kind == "g":
                 nc.sync.dma_start(out=raw_i[:], in_=g_rows[P * idx : P * (idx + 1), :])
@@ -67,7 +67,7 @@ def tile_locallyconnected2d_t_kernel(tc, inputs, kernel, bias, grad_out, out):
         dest = {}
         for t in range(4):
             for first_place in range(0, PLACES, PLACES_PER_STORE[t]):
-                o = outp.tile([P, PLACES_PER_STORE[t] * CIN], F32, name="out%d_%d" % (t, first_place))
+                o = outp.tile([P, PLACES_PER_STORE[t] * CIN], F32, name="out%d_%d" % (t, first_place), align_bytes=256)
                 for s in range(PLACES_PER_STORE[t]):
                     dest[(t, first_place + s)] = (o, s * CIN)
 

@@ -45,7 +45,7 @@ def tile_locallyconnected2d_t_kernel(tc, inputs, kernel, bias, grad_out, out):
 
         raw, codes, scales = [], [], []
         for i, (kind, idx) in enumerate(units):
-            raw_i = rawp.tile([P, 4 * UNIT_ROWS], BF16, name="raw%d" % i, align_bytes=256)
+            raw_i = rawp.tile([P, 4 * UNIT_ROWS], BF16, name="raw%d" % i, align_bytes=4096, offset=4096 * i)
             raw.append(raw_i)
             if kind == "g":
                 nc.sync.dma_start(out=raw_i[:], in_=g_rows[P * idx : P * (idx + 1), :])
@@ -67,7 +67,13 @@ def tile_locallyconnected2d_t_kernel(tc, inputs, kernel, bias, grad_out, out):
         dest = {}
         for t in range(4):
             for first_place in range(0, PLACES, PLACES_PER_STORE[t]):
-                o = outp.tile([P, PLACES_PER_STORE[t] * CIN], F32, name="out%d_%d" % (t, first_place), align_bytes=256)
+                o = outp.tile(
+                    [P, PLACES_PER_STORE[t] * CIN],
+                    F32,
+                    name="out%d_%d" % (t, first_place),
+                    align_bytes=4096,
+                    offset=4 * CIN * (PLACES * t + first_place),
+                )
                 for s in range(PLACES_PER_STORE[t]):
                     dest[(t, first_place + s)] = (o, s * CIN)
 

from contextlib import ExitStack

import concourse.mybir as mybir
from concourse.masks import make_identity

F32 = mybir.dt.float32
BF16 = mybir.dt.bfloat16
U32 = mybir.dt.uint32
U8 = mybir.dt.uint8
E4M3X4 = mybir.dt.float8_e4m3fn_x4
E5M2X4 = mybir.dt.float8_e5m2_x4

P = 128
B, PLACES, CIN, COUT = 512, 4, 1024, 512
FLOPS = 2 * PLACES * B * CIN * COUT
BYTES = 2 * B * PLACES * COUT + 2 * PLACES * CIN * COUT + 4 * B * PLACES * CIN

PIN = True
PLACES_PER_STORE = (1, 1, 2, 4)
UNIT_ROWS = 512


def tile_locallyconnected2d_t_kernel(tc, inputs, kernel, bias, grad_out, out):
    nc = tc.nc
    g_rows = grad_out.rearrange("b i j o -> b (i j o)")
    k_blocks = kernel.rearrange("i j c k l o -> (i j) c (k l) o")
    out_rows = out.rearrange("b i j c -> b (i j c)")

    units = [("g", 0), ("g", 1)] + [("k", h) for h in range(8)] + [("g", 2), ("g", 3)]
    n = len(units)
    unit_of = {}
    for i, u in enumerate(units):
        unit_of[u] = i

    with ExitStack() as ctx:
        if PIN:
            ctx.enter_context(tc.manual_schedule())
        const = ctx.enter_context(tc.tile_pool(name="const", bufs=1))
        rawp = ctx.enter_context(tc.tile_pool(name="rawp", bufs=1))
        keep = ctx.enter_context(tc.tile_pool(name="keep", bufs=1))
        stage = ctx.enter_context(tc.tile_pool(name="stage", bufs=4))
        outp = ctx.enter_context(tc.tile_pool(name="outp", bufs=1))
        tpsum = ctx.enter_context(tc.psum_pool(name="tpsum", bufs=4))
        mpsum = ctx.enter_context(tc.psum_pool(name="mpsum", bufs=4))

        raw, codes, scales = [], [], []
        for i, (kind, idx) in enumerate(units):
            raw_i = rawp.tile([P, 4 * UNIT_ROWS], BF16, name="raw%d" % i, align_bytes=4096, offset=4096 * i)
            raw.append(raw_i)
            if kind == "g":
                nc.sync.dma_start(out=raw_i[:], in_=g_rows[P * idx : P * (idx + 1), :])
            else:
                place, half = divmod(idx, 2)
                rows = k_blocks[place, UNIT_ROWS * half : UNIT_ROWS * (half + 1), place, :]
                nc.sync.dma_start(
                    out=raw_i[:].rearrange("q (t o) -> q t o", t=4),
                    in_=rows.rearrange("(t q) o -> q t o", q=P),
                )
            codes_i = keep.tile([P, UNIT_ROWS], U32, name="codes%d" % i, align_bytes=64)
            scales_i = keep.tile([P, UNIT_ROWS], U8, name="scales%d" % i, align_bytes=64)
            codes.append(codes_i)
            scales.append(scales_i)

        ident = const.tile([P, P], F32, name="ident")
        make_identity(nc, ident[:])

        dest = {}
        for t in range(4):
            for first_place in range(0, PLACES, PLACES_PER_STORE[t]):
                o = outp.tile(
                    [P, PLACES_PER_STORE[t] * CIN],
                    F32,
                    name="out%d_%d" % (t, first_place),
                    align_bytes=4096,
                    offset=4 * CIN * (PLACES * t + first_place),
                )
                for s in range(PLACES_PER_STORE[t]):
                    dest[(t, first_place + s)] = (o, s * CIN)

        booked = {"v": 0, "s": 0}

        def copy_out(dst, src, engine=None):
            if engine is None:
                engine = "s" if booked["s"] <= booked["v"] else "v"
            booked[engine] = booked[engine] + 1
            if engine == "v":
                nc.vector.tensor_copy(out=dst, in_=src)
            else:
                nc.scalar.copy(out=dst, in_=src)

        grouped_of = {}

        def prep(i):
            words = raw[i][:].bitcast(F32)
            grouped = stage.tile([P, 4 * UNIT_ROWS], BF16, name="grouped", tag="grouped", align_bytes=64)
            grouped_of[i] = grouped
            gw = grouped[:].bitcast(F32).rearrange("p (r u) -> p r u", u=2)
            for j in range(2):
                xt = tpsum.tile([P, 2, 2 * P], F32, name="xt", tag="xt")
                for s in range(2):
                    for u in range(2):
                        first = 256 * (2 * j + s) + P * u
                        nc.tensor.transpose(xt[:, u, P * s : P * (s + 1)], words[:, first : first + P], ident[:])
                copy_out(gw[:, 256 * j : 256 * (j + 1), :], xt[:].rearrange("p u r -> p r u"), "v" if j == 0 else "s")

        def quantise(i):
            fmt = E5M2X4 if units[i][0] == "g" else E4M3X4
            booked["v"] = booked["v"] + 1
            nc.vector.quantize_mx(out=codes[i][:].bitcast(fmt), scales=scales[i][:], in_=grouped_of[i][:])

        def product(t, h):
            gi, ki = unit_of[("g", t)], unit_of[("k", h)]
            place, half = divmod(h, 2)
            cols = slice(P * place, P * (place + 1))
            acc = mpsum.tile([P, UNIT_ROWS], F32, name="acc", tag="acc")
            nc.tensor.matmul_mx(
                out=acc[:],
                lhsT=codes[gi][:, cols].bitcast(E5M2X4),
                lhsT_scale=scales[gi][:, cols],
                rhs=codes[ki][:].bitcast(E4M3X4),
                rhs_scale=scales[ki][:],
                start=True,
                stop=True,
            )
            o, first = dest[(t, place)]
            first = first + UNIT_ROWS * half
            copy_out(o[:, first : first + UNIT_ROWS], acc[:])
            if first + UNIT_ROWS == o.shape[1]:
                last = (place + 1) * CIN
                nc.sync.dma_start(out=out_rows[P * t : P * (t + 1), last - o.shape[1] : last], in_=o[:])

        def products_after(i):
            kind, idx = units[i]
            if kind == "k":
                for t in range(2):
                    product(t, idx)
            elif idx >= 2:
                for h in range(8):
                    product(idx, h)

        for i in range(n + 2):
            if i < n:
                prep(i)
            if 1 <= i <= n:
                quantise(i - 1)
            if i >= 2:
                products_after(i - 2)
